import numpy as np
import ml_dtypes


BF16 = ml_dtypes.bfloat16


def bf(x):
    return np.asarray(x, np.float32).astype(BF16)


def f64(x):
    return np.asarray(x).astype(np.float64)


E2M1 = np.array([0.0, 0.5, 1.0, 1.5, 2.0, 3.0, 4.0, 6.0, -0.0, -0.5, -1.0, -1.5, -2.0, -3.0, -4.0, -6.0])


def pack_weight(w, fmt):
    k, n = w.shape
    w = f64(bf(w)).reshape(k // 32, 32, n)
    amax = np.abs(w).max(1)
    if fmt == "e4m3":
        byte = np.frexp(amax)[1] - 1 + 127 - 7
    else:
        mant, ex = np.frexp(amax / 6.0)
        byte = np.where(mant > 0.5, ex, ex - 1) + 127
    byte = np.clip(np.where(amax > 0, byte, 1), 1, 254)
    scaled = (w * np.exp2(127.0 - byte)[:, None, :]).reshape(k, n).astype(np.float32)
    by_word = np.ascontiguousarray(scaled.reshape(k // 512, 128, 4, n).transpose(0, 1, 3, 2))
    if fmt == "e4m3":
        words = by_word.astype(ml_dtypes.float8_e4m3fn).view(np.uint8)
    else:
        c = by_word.astype(ml_dtypes.float4_e2m1fn).view(np.uint8) & 0xF
        words = c[..., 0::2] | (c[..., 1::2] << 4)
    return np.ascontiguousarray(words), np.ascontiguousarray(byte.astype(np.uint8).reshape(k // 512, 16, n))


def unpack_weight(words, scales, fmt):
    g, p, n, _ = words.shape
    if fmt == "e4m3":
        vals = np.ascontiguousarray(words).view(ml_dtypes.float8_e4m3fn).astype(np.float64)
    else:
        nib = np.empty((g, p, n, 4), np.uint8)
        nib[..., 0::2] = words & 0xF
        nib[..., 1::2] = words >> 4
        vals = E2M1[nib]
    vals = vals * np.repeat(np.exp2(scales.astype(np.float64) - 127.0), 8, axis=1)[..., None]
    return vals.transpose(0, 1, 3, 2).reshape(g * 512, n)

def pack4(w):
    words, scales = pack_weight(w, "e2m1")
    return words.reshape(words.shape[0], 128, -1), scales


def unpack4(words, scales):
    return unpack_weight(words.reshape(words.shape[0], 128, -1, 2), scales, "e2m1")


def kspread(k):
    return np.exp2(np.repeat(np.random.randint(-6, 7, k // 32), 32).astype(np.float64))


S, B, H, NH, HD, ROT = 1536, 1, 2048, 16, 128, 32
BASE = 10000.0
W3 = 3 * NH * HD


def rotate_half(x):
    x1, x2 = np.split(x, 2, axis=-1)
    return np.concatenate((-x2, x1), axis=-1)


def setup_inputs():
    s = kspread(H)
    hidden_states = np.random.standard_normal((S, B, H)) * s
    hidden_states_words, hidden_states_scales = pack4(hidden_states.reshape(S * B, H).T)
    words, scales = pack4((np.random.standard_normal((W3, H)) / np.sqrt(H) / s[None, :]).T)
    return {"hidden_states_words": hidden_states_words,
            "hidden_states_scales": hidden_states_scales,
            "W_qkv_words": words,
            "W_qkv_scales": scales,
            "b_qkv": bf(np.random.standard_normal(W3) * 0.2)}


def reference(hidden_states_words, hidden_states_scales, W_qkv_words, W_qkv_scales, b_qkv):
    x = unpack4(hidden_states_words, hidden_states_scales).T.reshape(S, B, H)
    S_, B_ = x.shape[:2]
    qkv = (x @ unpack4(W_qkv_words, W_qkv_scales)) + f64(b_qkv)
    qkv = qkv.reshape(S_, B_, NH, 3 * HD)
    q, k, v = qkv[..., :HD], qkv[..., HD:2 * HD], qkv[..., 2 * HD:]

    inv_freq = 1.0 / (BASE ** (np.arange(0, ROT, 2) / ROT))
    t = np.arange(S_)
    freqs = t[:, None] * inv_freq[None, :]
    emb = np.concatenate((freqs, freqs), axis=-1)
    cos = np.cos(emb)[:, None, None, :]
    sin = np.sin(emb)[:, None, None, :]

    def rope(u):
        return u * cos + rotate_half(u) * sin

    q = np.concatenate((rope(q[..., :ROT]), q[..., ROT:]), axis=-1)
    k = np.concatenate((rope(k[..., :ROT]), k[..., ROT:]), axis=-1)
    return q, k, v

@@ -1,0 +1,266 @@
+from contextlib import ExitStack
+import math
+
+import concourse.mybir as mybir
+from concourse.masks import make_identity
+
+SEQ, HID, NH, HD, ROT = 1536, 2048, 16, 128, 32
+BASE = 10000.0
+FLOPS = 2 * SEQ * HID * 3 * NH * HD
+
+F32 = mybir.dt.float32
+BF16 = mybir.dt.bfloat16
+I32 = mybir.dt.int32
+U8 = mybir.dt.uint8
+FP4X4 = mybir.dt.float4_e2m1fn_x4
+ALU = mybir.AluOpType
+ACT = mybir.ActivationFunctionType
+
+P = 128
+G = HID // 512
+MT = SEQ // P
+NI = 4
+HG = NH // NI
+UW = 3 * HG * HD
+NB = UW // 512
+HALF = ROT // 2
+
+TWO_PI = 2.0 * math.pi
+C1 = 6.28125
+C2 = TWO_PI - C1
+
+X_SPLIT = ((0, 4), (4, 12))
+S_BUFS = 12
+MG = 4
+TAIL = 3
+
+
+def tile_selfattention_pa_kernel(
+    tc, hidden_states_words, hidden_states_scales, W_qkv_words, W_qkv_scales, b_qkv, out_0, out_1, out_2
+):
+    nc = tc.nc
+    outs = [o.rearrange("s b h d -> (s b) (h d)") for o in (out_0, out_1, out_2)]
+
+    with ExitStack() as ctx:
+        keep = ctx.enter_context(tc.tile_pool(name="keep", bufs=1))
+        spool = ctx.enter_context(tc.tile_pool(name="spool", bufs=S_BUFS))
+        tpool = ctx.enter_context(tc.tile_pool(name="tpool", bufs=2))
+        psum = ctx.enter_context(tc.psum_pool(name="psum", bufs=8))
+        ctx.enter_context(tc.manual_schedule())
+
+        x_codes = [keep.tile([P, G, 256 * (m1 - m0)], U8, name="xc%d" % n, align_bytes=64)
+                   for n, (m0, m1) in enumerate(X_SPLIT)]
+        x_planes = [keep.tile([P, G, 128 * (m1 - m0)], U8, name="xp%d" % n, align_bytes=64)
+                    for n, (m0, m1) in enumerate(X_SPLIT)]
+        w0_codes = [keep.tile([P, G, 1024], U8, name="w0c%d" % b, align_bytes=64) for b in range(NB)]
+        w0_planes = [keep.tile([P, G, 512], U8, name="w0p%d" % b, align_bytes=64) for b in range(NB)]
+        w_codes = [None] + [keep.tile([P, G, 2 * UW], U8, name="wc%d" % i, align_bytes=64) for i in range(1, NI)]
+        w_planes = [None] + [keep.tile([P, G, UW], U8, name="wp%d" % i, align_bytes=64) for i in range(1, NI)]
+        bias = [keep.tile([P, UW], F32, name="bias0")] + [keep.tile([P, UW], BF16, name="bias%d" % i) for i in range(1, NI)]
+        b_rows = keep.tile([P, 512], BF16, name="b_rows")
+        ident = keep.tile([P, P], BF16, name="ident")
+        pos_i = keep.tile([P, MT], I32, name="pos_i")
+
+        def load_codes(dst, src, c0, c1):
+            nc.sync.dma_start(
+                out=dst[:].bitcast(I32),
+                in_=src[:, :, c0:c1].rearrange("g p n -> p g n").bitcast(I32),
+            )
+
+        def load_planes(dst, src, c0, c1):
+            for q in range(4):
+                nc.sync.dma_start(
+                    out=dst[32 * q : 32 * q + 4, :, :].bitcast(I32),
+                    in_=src[:, 4 * q : 4 * q + 4, c0:c1].rearrange("g r n -> r g n").bitcast(I32),
+                )
+
+        nc.vector.memset(b_rows[:], 0.0)
+        for t in (x_planes[0], w0_planes[0], w0_planes[1], w0_planes[2], x_planes[1]):
+            nc.vector.memset(t[:].bitcast(I32), 0)
+        nc.gpsimd.iota(pos_i[:], pattern=[[P, MT]], base=0, channel_multiplier=1)
+        make_identity(nc, ident[:])
+        for i in range(1, NI):
+            nc.gpsimd.memset(w_planes[i][:].bitcast(F32), 0.0)
+
+        def load_bias(i):
+            nc.gpsimd.dma_start(out=bias[i][:], in_=b_qkv[UW * i : UW * (i + 1)].partition_broadcast(P))
+
+        load_bias(1)
+
+        nc.scalar.dma_start(out=b_rows[0:4, :], in_=b_qkv[0:2048].rearrange("(n c) -> n c", c=512))
+        load_codes(x_codes[0], hidden_states_words, 0, 256 * 4)
+        load_codes(w0_codes[0], W_qkv_words, 0, 1024)
+        load_planes(x_planes[0], hidden_states_scales, 0, 128 * 4)
+        load_planes(w0_planes[0], W_qkv_scales, 0, 512)
+        load_planes(w0_planes[1], W_qkv_scales, 512, 1024)
+        load_codes(w0_codes[1], W_qkv_words, 1024, 2048)
+        load_planes(w0_planes[2], W_qkv_scales, 1024, 1536)
+        load_codes(w0_codes[2], W_qkv_words, 2048, 3072)
+        load_planes(x_planes[1], hidden_states_scales, 128 * 4, 128 * 12)
+        load_codes(x_codes[1], hidden_states_words, 256 * 4, 256 * 12)
+        for i in range(1, NI):
+            load_planes(w_planes[i], W_qkv_scales, UW * i, UW * (i + 1))
+        for i in range(1, NI):
+            load_codes(w_codes[i], W_qkv_words, 2 * UW * i, 2 * UW * (i + 1))
+
+        for b in range(NB):
+            acc = psum.tile([P, 512], F32, name="acc")
+            nc.tensor.matmul(out=acc[:], lhsT=ident[:, b : b + 1].to_broadcast([P, P]), rhs=b_rows[:], start=True, stop=True)
+            nc.scalar.copy(out=bias[0][:, 512 * b : 512 * (b + 1)], in_=acc[:])
+
+        pos = keep.tile([P, MT], F32, name="pos")
+        nc.vector.tensor_copy(out=pos[:], in_=pos_i[:])
+        ang = keep.tile([P, MT, HALF], F32, name="ang")
+        for j in range(HALF):
+            nc.vector.tensor_scalar(
+                out=ang[:, :, j], in0=pos[:], scalar1=BASE ** (-j / float(HALF)), scalar2=None, op0=ALU.mult
+            )
+        turns_i = keep.tile([P, MT, HALF], I32, name="turns_i")
+        nc.vector.tensor_scalar(out=turns_i[:], in0=ang[:], scalar1=1.0 / TWO_PI, scalar2=None, op0=ALU.mult)
+        turns = keep.tile([P, MT, HALF], F32, name="turns")
+        nc.vector.tensor_copy(out=turns[:], in_=turns_i[:])
+        red1 = keep.tile([P, MT, HALF], F32, name="red1")
+        nc.vector.scalar_tensor_tensor(out=red1[:], in0=turns[:], scalar=-C1, in1=ang[:], op0=ALU.mult, op1=ALU.add)
+        red2 = keep.tile([P, MT, HALF], F32, name="red2")
+        nc.vector.scalar_tensor_tensor(out=red2[:], in0=turns[:], scalar=-C2, in1=red1[:], op0=ALU.mult, op1=ALU.add)
+
+        def wrapped(src, name, bound, op, shift):
+            fix = keep.tile([P, MT, HALF], F32, name=name + "f")
+            nc.vector.tensor_scalar(out=fix[:], in0=src[:], scalar1=bound, scalar2=shift, op0=op, op1=ALU.mult)
+            res = keep.tile([P, MT, HALF], F32, name=name)
+            nc.vector.tensor_tensor(out=res[:], in0=src[:], in1=fix[:], op=ALU.add)
+            return res
+
+        arg_sin = wrapped(wrapped(red2, "sa", math.pi, ALU.is_gt, -TWO_PI), "sb", -math.pi, ALU.is_lt, TWO_PI)
+        shifted = keep.tile([P, MT, HALF], F32, name="shifted")
+        nc.vector.tensor_scalar(out=shifted[:], in0=arg_sin[:], scalar1=0.5 * math.pi, scalar2=None, op0=ALU.add)
+        arg_cos = wrapped(shifted, "ca", math.pi, ALU.is_gt, -TWO_PI)
+
+        tab = keep.tile([P, MT, 2, ROT], F32, name="tab")
+        nc.scalar.activation(out=tab[:, :, 0, 0:HALF], in_=arg_cos[:], func=ACT.Sin)
+        nc.scalar.activation(out=tab[:, :, 0, HALF:ROT], in_=arg_cos[:], func=ACT.Sin)
+        nc.scalar.activation(out=tab[:, :, 1, 0:HALF], in_=arg_sin[:], func=ACT.Sin)
+        nc.scalar.activation(out=tab[:, :, 1, HALF:ROT], in_=arg_sin[:], func=ACT.Sin, scale=-1.0)
+
+        def multiply(out, i, m, c0, width):
+            n = 0 if m < X_SPLIT[0][1] else 1
+            mm = m - X_SPLIT[n][0]
+            for g in range(G):
+                if i == 0:
+                    wc = w0_codes[c0 // 512][:, g, 2 * (c0 % 512) : 2 * (c0 % 512 + width)]
+                    wp = w0_planes[c0 // 512][:, g, c0 % 512 : c0 % 512 + width]
+                else:
+                    wc = w_codes[i][:, g, 2 * c0 : 2 * (c0 + width)]
+                    wp = w_planes[i][:, g, c0 : c0 + width]
+                nc.tensor.matmul_mx(
+                    out=out,
+                    lhsT=x_codes[n][:, g, 256 * mm : 256 * (mm + 1)].bitcast(FP4X4),
+                    lhsT_scale=x_planes[n][:, g, 128 * mm : 128 * (mm + 1)],
+                    rhs=wc.bitcast(FP4X4),
+                    rhs_scale=wp,
+                    start=(g == 0),
+                    stop=(g == G - 1),
+                )
+
+        stage = {}
+
+        def staging(i, m):
+            if (i, m) not in stage:
+                stage[(i, m)] = spool.tile([P, 3, HG, HD], F32, name="st")
+            return stage[(i, m)]
+
+        def block(i, m, b):
+            acc = psum.tile([P, 512], F32, name="acc")
+            multiply(acc[:], i, m, 512 * b, 512)
+            st = staging(i, m)
+            s = 0
+            for step in range(4):
+                if s < 4:
+                    h, c = divmod(4 * b + s, 3)
+                    n = min(3 - c, 4 - s)
+                    nc.vector.tensor_tensor(
+                        out=st[:, c : c + n, h, :],
+                        in0=acc[:, HD * s : HD * (s + n)].rearrange("p (c d) -> p c d", c=n),
+                        in1=bias[i][:, 512 * b + HD * s : 512 * b + HD * (s + n)].rearrange("p (c d) -> p c d", c=n),
+                        op=ALU.add,
+                    )
+                    s += n
+
+        def rotate(i, m):
+            st = staging(i, m)
+            rot = st[:, 0:2, :, :].rearrange("p c h d -> p (c h) d")[:, :, 0:ROT]
+            prod = tpool.tile([P, 2 * HG, 2, ROT], F32, name="prod")
+            nc.gpsimd.tensor_tensor(
+                out=prod[:],
+                in0=rot.unsqueeze(2).to_broadcast([P, 2 * HG, 2, ROT]),
+                in1=tab[:, m, :, :].unsqueeze(1).to_broadcast([P, 2 * HG, 2, ROT]),
+                op=ALU.mult,
+            )
+            nc.gpsimd.tensor_tensor(
+                out=rot[:, :, 0:HALF], in0=prod[:, :, 0, 0:HALF], in1=prod[:, :, 1, HALF:ROT], op=ALU.add
+            )
+            nc.gpsimd.tensor_tensor(
+                out=rot[:, :, HALF:ROT], in0=prod[:, :, 0, HALF:ROT], in1=prod[:, :, 1, 0:HALF], op=ALU.add
+            )
+
+        def store(queue, i, m, c, h0, h1):
+            nc_rows = slice(P * m, P * (m + 1))
+            queue.dma_start(
+                out=outs[c][nc_rows, HD * (HG * i + h0) : HD * (HG * i + h1)],
+                in_=staging(i, m)[:, c, h0:h1, :].rearrange("p h d -> p (h d)"),
+            )
+
+        def finish(i, m):
+            rotate(i, m)
+            if m == 0 and i + 2 < NI:
+                load_bias(i + 2)
+            store(nc.sync, i, m, 2, 0, HG)
+            store(nc.scalar, i, m, 0, 0, HG)
+            store(nc.scalar, i, m, 1, 0, HG)
+
+        def by_head(ap, h0):
+            return ap[:, 3 * HD * h0 : 3 * HD * (h0 + 2)].rearrange("p (h x) -> p h x", h=2)
+
+        def qk_pair(i, m, h0):
+            acc = psum.tile([P, 512], F32, name="acc")
+            for hh in range(2):
+                multiply(acc[:, 256 * hh : 256 * (hh + 1)], i, m, 3 * HD * (h0 + hh), 2 * HD)
+            nc.vector.tensor_tensor(
+                out=staging(i, m)[:, 0:2, h0 : h0 + 2, :].rearrange("p c h d -> p h c d"),
+                in0=acc[:].rearrange("p (h c d) -> p h c d", h=2, c=2),
+                in1=by_head(bias[i], h0)[:, :, 0 : 2 * HD].rearrange("p h (c d) -> p h c d", c=2),
+                op=ALU.add,
+            )
+
+        def v_pair(i, m, h0):
+            acc = psum.tile([P, 512], F32, name="acc")
+            for hh in range(2):
+                multiply(acc[:, HD * hh : HD * (hh + 1)], i, m, 3 * HD * (h0 + hh) + 2 * HD, HD)
+            nc.vector.tensor_tensor(
+                out=staging(i, m)[:, 2, h0 : h0 + 2, :],
+                in0=acc[:, 0 : 2 * HD].rearrange("p (h d) -> p h d", h=2),
+                in1=by_head(bias[i], h0)[:, :, 2 * HD : 3 * HD],
+                op=ALU.add,
+            )
+            store(nc.sync, i, m, 2, h0, h0 + 2)
+
+        for m0 in range(0, MT, MG):
+            for b in range(NB):
+                for m in range(m0, m0 + MG):
+                    block(0, m, b)
+                    if b == NB - 1:
+                        finish(0, m)
+        for i in range(1, NI):
+            for m in range(MT - TAIL if i == NI - 1 else MT):
+                for b in range(NB):
+                    block(i, m, b)
+                finish(i, m)
+        for m in range(MT - TAIL, MT):
+            for h0 in range(0, HG, 2):
+                qk_pair(NI - 1, m, h0)
+            rotate(NI - 1, m)
+            store(nc.scalar, NI - 1, m, 0, 0, HG)
+            store(nc.scalar, NI - 1, m, 1, 0, HG)
+        for m in range(MT - TAIL, MT):
+            for h0 in range(0, HG, 2):
+                v_pair(NI - 1, m, h0)

@@ -29,8 +29,9 @@ TWO_PI = 2.0 * math.pi
 C1 = 6.28125
 C2 = TWO_PI - C1
 
-X_SPLIT = ((0, 4), (4, 12))
-S_BUFS = 12
+X_SPLIT = ((0, 2), (2, 4), (4, 12))
+XP_SPLIT = ((0, 4), (4, 12))
+S_BUFS = 16
 MG = 4
 TAIL = 3
 
@@ -51,8 +52,9 @@ def tile_selfattention_pa_kernel(
         x_codes = [keep.tile([P, G, 256 * (m1 - m0)], U8, name="xc%d" % n, align_bytes=64)
                    for n, (m0, m1) in enumerate(X_SPLIT)]
         x_planes = [keep.tile([P, G, 128 * (m1 - m0)], U8, name="xp%d" % n, align_bytes=64)
-                    for n, (m0, m1) in enumerate(X_SPLIT)]
-        w0_codes = [keep.tile([P, G, 1024], U8, name="w0c%d" % b, align_bytes=64) for b in range(NB)]
+                    for n, (m0, m1) in enumerate(XP_SPLIT)]
+        w0_codes = [None] + [keep.tile([P, G, 1024], U8, name="w0c%d" % b, align_bytes=64) for b in range(1, NB)]
+        w00_codes = [keep.tile([P, 2, 1024], U8, name="w00c%d" % n, align_bytes=64) for n in range(2)]
         w0_planes = [keep.tile([P, G, 512], U8, name="w0p%d" % b, align_bytes=64) for b in range(NB)]
         w_codes = [None] + [keep.tile([P, G, 2 * UW], U8, name="wc%d" % i, align_bytes=64) for i in range(1, NI)]
         w_planes = [None] + [keep.tile([P, G, UW], U8, name="wp%d" % i, align_bytes=64) for i in range(1, NI)]
@@ -61,10 +63,10 @@ def tile_selfattention_pa_kernel(
         ident = keep.tile([P, P], BF16, name="ident")
         pos_i = keep.tile([P, MT], I32, name="pos_i")
 
-        def load_codes(dst, src, c0, c1):
+        def load_codes(dst, src, c0, c1, g0=0, g1=G):
             nc.sync.dma_start(
                 out=dst[:].bitcast(I32),
-                in_=src[:, :, c0:c1].rearrange("g p n -> p g n").bitcast(I32),
+                in_=src[g0:g1, :, c0:c1].rearrange("g p n -> p g n").bitcast(I32),
             )
 
         def load_planes(dst, src, c0, c1):
@@ -74,7 +76,7 @@ def tile_selfattention_pa_kernel(
                     in_=src[:, 4 * q : 4 * q + 4, c0:c1].rearrange("g r n -> r g n").bitcast(I32),
                 )
 
-        nc.vector.memset(b_rows[:], 0.0)
+        nc.gpsimd.memset(b_rows[:], 0.0)
         for t in (x_planes[0], w0_planes[0], w0_planes[1], w0_planes[2], x_planes[1]):
             nc.vector.memset(t[:].bitcast(I32), 0)
         nc.gpsimd.iota(pos_i[:], pattern=[[P, MT]], base=0, channel_multiplier=1)
@@ -88,16 +90,18 @@ def tile_selfattention_pa_kernel(
         load_bias(1)
 
         nc.scalar.dma_start(out=b_rows[0:4, :], in_=b_qkv[0:2048].rearrange("(n c) -> n c", c=512))
-        load_codes(x_codes[0], hidden_states_words, 0, 256 * 4)
-        load_codes(w0_codes[0], W_qkv_words, 0, 1024)
+        load_codes(x_codes[0], hidden_states_words, 0, 256 * 2)
+        load_codes(w00_codes[0], W_qkv_words, 0, 1024, 0, 2)
         load_planes(x_planes[0], hidden_states_scales, 0, 128 * 4)
         load_planes(w0_planes[0], W_qkv_scales, 0, 512)
+        load_codes(w00_codes[1], W_qkv_words, 0, 1024, 2, 4)
+        load_codes(x_codes[1], hidden_states_words, 256 * 2, 256 * 4)
         load_planes(w0_planes[1], W_qkv_scales, 512, 1024)
         load_codes(w0_codes[1], W_qkv_words, 1024, 2048)
         load_planes(w0_planes[2], W_qkv_scales, 1024, 1536)
         load_codes(w0_codes[2], W_qkv_words, 2048, 3072)
         load_planes(x_planes[1], hidden_states_scales, 128 * 4, 128 * 12)
-        load_codes(x_codes[1], hidden_states_words, 256 * 4, 256 * 12)
+        load_codes(x_codes[2], hidden_states_words, 256 * 4, 256 * 12)
         for i in range(1, NI):
             load_planes(w_planes[i], W_qkv_scales, UW * i, UW * (i + 1))
         for i in range(1, NI):
@@ -143,10 +147,15 @@ def tile_selfattention_pa_kernel(
         nc.scalar.activation(out=tab[:, :, 1, HALF:ROT], in_=arg_sin[:], func=ACT.Sin, scale=-1.0)
 
         def multiply(out, i, m, c0, width):
-            n = 0 if m < X_SPLIT[0][1] else 1
+            n = [k for k, (m0, m1) in enumerate(X_SPLIT) if m0 <= m < m1][0]
             mm = m - X_SPLIT[n][0]
+            np_ = [k for k, (m0, m1) in enumerate(XP_SPLIT) if m0 <= m < m1][0]
+            mp = m - XP_SPLIT[np_][0]
             for g in range(G):
-                if i == 0:
+                if i == 0 and c0 == 0:
+                    wc = w00_codes[g // 2][:, g % 2, :]
+                    wp = w0_planes[0][:, g, :]
+                elif i == 0:
                     wc = w0_codes[c0 // 512][:, g, 2 * (c0 % 512) : 2 * (c0 % 512 + width)]
                     wp = w0_planes[c0 // 512][:, g, c0 % 512 : c0 % 512 + width]
                 else:
@@ -155,7 +164,7 @@ def tile_selfattention_pa_kernel(
                 nc.tensor.matmul_mx(
                     out=out,
                     lhsT=x_codes[n][:, g, 256 * mm : 256 * (mm + 1)].bitcast(FP4X4),
-                    lhsT_scale=x_planes[n][:, g, 128 * mm : 128 * (mm + 1)],
+                    lhsT_scale=x_planes[np_][:, g, 128 * mp : 128 * (mp + 1)],
                     rhs=wc.bitcast(FP4X4),
                     rhs_scale=wp,
                     start=(g == 0),

@@ -24,13 +24,14 @@ HG = NH // NI
 UW = 3 * HG * HD
 NB = UW // 512
 HALF = ROT // 2
+BW = 3 * NH * HD // 32
 
 TWO_PI = 2.0 * math.pi
 C1 = 6.28125
 C2 = TWO_PI - C1
 
 X_SPLIT = ((0, 2), (2, 4), (4, 12))
-XP_SPLIT = ((0, 4), (4, 12))
+XP_SPLIT = ((0, 2), (2, 4), (4, 12))
 S_BUFS = 16
 MG = 4
 TAIL = 3
@@ -59,7 +60,7 @@ def tile_selfattention_pa_kernel(
         w_codes = [None] + [keep.tile([P, G, 2 * UW], U8, name="wc%d" % i, align_bytes=64) for i in range(1, NI)]
         w_planes = [None] + [keep.tile([P, G, UW], U8, name="wp%d" % i, align_bytes=64) for i in range(1, NI)]
         bias = [keep.tile([P, UW], F32, name="bias0")] + [keep.tile([P, UW], BF16, name="bias%d" % i) for i in range(1, NI)]
-        b_rows = keep.tile([P, 512], BF16, name="b_rows")
+        b_rows = keep.tile([P, BW], BF16, name="b_rows")
         ident = keep.tile([P, P], BF16, name="ident")
         pos_i = keep.tile([P, MT], I32, name="pos_i")
 
@@ -69,18 +70,20 @@ def tile_selfattention_pa_kernel(
                 in_=src[g0:g1, :, c0:c1].rearrange("g p n -> p g n").bitcast(I32),
             )
 
-        def load_planes(dst, src, c0, c1):
-            for q in range(4):
+        def load_planes(dst, src, c0, c1, q0=0, q1=4):
+            for q in range(q0, q1):
                 nc.sync.dma_start(
                     out=dst[32 * q : 32 * q + 4, :, :].bitcast(I32),
                     in_=src[:, 4 * q : 4 * q + 4, c0:c1].rearrange("g r n -> r g n").bitcast(I32),
                 )
 
-        nc.gpsimd.memset(b_rows[:], 0.0)
-        for t in (x_planes[0], w0_planes[0], w0_planes[1], w0_planes[2], x_planes[1]):
+        nc.vector.memset(x_planes[0][:].bitcast(I32), 0)
+        nc.vector.memset(b_rows[32:64, :], 0.0)
+        nc.vector.memset(b_rows[64:128, :], 0.0)
+        for t in (w0_planes[0], x_planes[1], w0_planes[1], w0_planes[2], x_planes[2]):
             nc.vector.memset(t[:].bitcast(I32), 0)
-        nc.gpsimd.iota(pos_i[:], pattern=[[P, MT]], base=0, channel_multiplier=1)
         make_identity(nc, ident[:])
+        nc.gpsimd.iota(pos_i[:], pattern=[[P, MT]], base=0, channel_multiplier=1)
         for i in range(1, NI):
             nc.gpsimd.memset(w_planes[i][:].bitcast(F32), 0.0)
 
@@ -89,28 +92,37 @@ def tile_selfattention_pa_kernel(
 
         load_bias(1)
 
-        nc.scalar.dma_start(out=b_rows[0:4, :], in_=b_qkv[0:2048].rearrange("(n c) -> n c", c=512))
+        nc.sync.dma_start(out=b_rows[0:32, :], in_=b_qkv.rearrange("(n c) -> n c", c=BW))
+        load_planes(x_planes[0], hidden_states_scales, 0, 128 * 2, 0, 2)
         load_codes(x_codes[0], hidden_states_words, 0, 256 * 2)
         load_codes(w00_codes[0], W_qkv_words, 0, 1024, 0, 2)
-        load_planes(x_planes[0], hidden_states_scales, 0, 128 * 4)
+        load_planes(x_planes[0], hidden_states_scales, 0, 128 * 2, 2, 4)
         load_planes(w0_planes[0], W_qkv_scales, 0, 512)
         load_codes(w00_codes[1], W_qkv_words, 0, 1024, 2, 4)
         load_codes(x_codes[1], hidden_states_words, 256 * 2, 256 * 4)
+        load_planes(x_planes[1], hidden_states_scales, 128 * 2, 128 * 4)
         load_planes(w0_planes[1], W_qkv_scales, 512, 1024)
         load_codes(w0_codes[1], W_qkv_words, 1024, 2048)
         load_planes(w0_planes[2], W_qkv_scales, 1024, 1536)
         load_codes(w0_codes[2], W_qkv_words, 2048, 3072)
-        load_planes(x_planes[1], hidden_states_scales, 128 * 4, 128 * 12)
+        load_planes(x_planes[2], hidden_states_scales, 128 * 4, 128 * 12)
         load_codes(x_codes[2], hidden_states_words, 256 * 4, 256 * 12)
         for i in range(1, NI):
             load_planes(w_planes[i], W_qkv_scales, UW * i, UW * (i + 1))
         for i in range(1, NI):
             load_codes(w_codes[i], W_qkv_words, 2 * UW * i, 2 * UW * (i + 1))
 
-        for b in range(NB):
+        for b in range(UW // (2 * BW)):
             acc = psum.tile([P, 512], F32, name="acc")
-            nc.tensor.matmul(out=acc[:], lhsT=ident[:, b : b + 1].to_broadcast([P, P]), rhs=b_rows[:], start=True, stop=True)
-            nc.scalar.copy(out=bias[0][:, 512 * b : 512 * (b + 1)], in_=acc[:])
+            for e in range(2):
+                nc.tensor.matmul(
+                    out=acc[:, BW * e : BW * (e + 1)],
+                    lhsT=ident[:, 2 * b + e : 2 * b + e + 1].to_broadcast([P, P]),
+                    rhs=b_rows[:],
+                    start=True,
+                    stop=True,
+                )
+            nc.scalar.copy(out=bias[0][:, 2 * BW * b : 2 * BW * (b + 1)], in_=acc[:, 0 : 2 * BW])
 
         pos = keep.tile([P, MT], F32, name="pos")
         nc.vector.tensor_copy(out=pos[:], in_=pos_i[:])

@@ -84,13 +84,9 @@ def tile_selfattention_pa_kernel(
             nc.vector.memset(t[:].bitcast(I32), 0)
         make_identity(nc, ident[:])
         nc.gpsimd.iota(pos_i[:], pattern=[[P, MT]], base=0, channel_multiplier=1)
-        for i in range(1, NI):
-            nc.gpsimd.memset(w_planes[i][:].bitcast(F32), 0.0)
 
         def load_bias(i):
             nc.gpsimd.dma_start(out=bias[i][:], in_=b_qkv[UW * i : UW * (i + 1)].partition_broadcast(P))
-
-        load_bias(1)
 
         nc.sync.dma_start(out=b_rows[0:32, :], in_=b_qkv.rearrange("(n c) -> n c", c=BW))
         load_planes(x_planes[0], hidden_states_scales, 0, 128 * 2, 0, 2)
@@ -107,10 +103,6 @@ def tile_selfattention_pa_kernel(
         load_codes(w0_codes[2], W_qkv_words, 2048, 3072)
         load_planes(x_planes[2], hidden_states_scales, 128 * 4, 128 * 12)
         load_codes(x_codes[2], hidden_states_words, 256 * 4, 256 * 12)
-        for i in range(1, NI):
-            load_planes(w_planes[i], W_qkv_scales, UW * i, UW * (i + 1))
-        for i in range(1, NI):
-            load_codes(w_codes[i], W_qkv_words, 2 * UW * i, 2 * UW * (i + 1))
 
         for b in range(UW // (2 * BW)):
             acc = psum.tile([P, 512], F32, name="acc")
@@ -140,23 +132,32 @@ def tile_selfattention_pa_kernel(
         red2 = keep.tile([P, MT, HALF], F32, name="red2")
         nc.vector.scalar_tensor_tensor(out=red2[:], in0=turns[:], scalar=-C2, in1=red1[:], op0=ALU.mult, op1=ALU.add)
 
-        def wrapped(src, name, bound, op, shift):
+        def wrapped(eng, src, name, bound, op, shift):
             fix = keep.tile([P, MT, HALF], F32, name=name + "f")
-            nc.vector.tensor_scalar(out=fix[:], in0=src[:], scalar1=bound, scalar2=shift, op0=op, op1=ALU.mult)
+            eng.tensor_scalar(out=fix[:], in0=src[:], scalar1=bound, scalar2=shift, op0=op, op1=ALU.mult)
             res = keep.tile([P, MT, HALF], F32, name=name)
-            nc.vector.tensor_tensor(out=res[:], in0=src[:], in1=fix[:], op=ALU.add)
+            eng.tensor_tensor(out=res[:], in0=src[:], in1=fix[:], op=ALU.add)
             return res
 
-        arg_sin = wrapped(wrapped(red2, "sa", math.pi, ALU.is_gt, -TWO_PI), "sb", -math.pi, ALU.is_lt, TWO_PI)
+        arg_sin = wrapped(
+            nc.vector, wrapped(nc.vector, red2, "sa", math.pi, ALU.is_gt, -TWO_PI), "sb", -math.pi, ALU.is_lt, TWO_PI
+        )
         shifted = keep.tile([P, MT, HALF], F32, name="shifted")
-        nc.vector.tensor_scalar(out=shifted[:], in0=arg_sin[:], scalar1=0.5 * math.pi, scalar2=None, op0=ALU.add)
-        arg_cos = wrapped(shifted, "ca", math.pi, ALU.is_gt, -TWO_PI)
+        nc.gpsimd.tensor_scalar(out=shifted[:], in0=arg_sin[:], scalar1=1.0, scalar2=0.5 * math.pi, op0=ALU.mult, op1=ALU.add)
+        arg_cos = wrapped(nc.gpsimd, shifted, "ca", math.pi, ALU.is_gt, -TWO_PI)
+        load_bias(1)
+        for i in range(1, NI):
+            nc.gpsimd.memset(w_planes[i][:].bitcast(F32), 0.0)
+        for i in range(1, NI):
+            load_planes(w_planes[i], W_qkv_scales, UW * i, UW * (i + 1))
+        for i in range(1, NI):
+            load_codes(w_codes[i], W_qkv_words, 2 * UW * i, 2 * UW * (i + 1))
 
         tab = keep.tile([P, MT, 2, ROT], F32, name="tab")
-        nc.scalar.activation(out=tab[:, :, 0, 0:HALF], in_=arg_cos[:], func=ACT.Sin)
-        nc.scalar.activation(out=tab[:, :, 0, HALF:ROT], in_=arg_cos[:], func=ACT.Sin)
         nc.scalar.activation(out=tab[:, :, 1, 0:HALF], in_=arg_sin[:], func=ACT.Sin)
         nc.scalar.activation(out=tab[:, :, 1, HALF:ROT], in_=arg_sin[:], func=ACT.Sin, scale=-1.0)
+        nc.scalar.activation(out=tab[:, :, 0, 0:HALF], in_=arg_cos[:], func=ACT.Sin)
+        nc.scalar.activation(out=tab[:, :, 0, HALF:ROT], in_=arg_cos[:], func=ACT.Sin)
 
         def multiply(out, i, m, c0, width):
             n = [k for k, (m0, m1) in enumerate(X_SPLIT) if m0 <= m < m1][0]

@@ -34,6 +34,7 @@ X_SPLIT = ((0, 2), (2, 4), (4, 12))
 XP_SPLIT = ((0, 2), (2, 4), (4, 12))
 S_BUFS = 16
 MG = 4
+WARM_BEFORE, WARM_AFTER = 8, 14
 TAIL = 3
 
 
@@ -104,6 +105,12 @@ def tile_selfattention_pa_kernel(
         load_planes(x_planes[2], hidden_states_scales, 128 * 4, 128 * 12)
         load_codes(x_codes[2], hidden_states_words, 256 * 4, 256 * 12)
 
+        def keep_busy(n):
+            idle = psum.tile([P, 512], F32, name="acc")
+            for k in range(n):
+                nc.tensor.matmul(out=idle[:, 0:P], lhsT=ident[:], rhs=ident[:], start=True, stop=True)
+
+        keep_busy(WARM_BEFORE)
         for b in range(UW // (2 * BW)):
             acc = psum.tile([P, 512], F32, name="acc")
             for e in range(2):
@@ -115,6 +122,7 @@ def tile_selfattention_pa_kernel(
                     stop=True,
                 )
             nc.scalar.copy(out=bias[0][:, 2 * BW * b : 2 * BW * (b + 1)], in_=acc[:, 0 : 2 * BW])
+        keep_busy(WARM_AFTER)
 
         pos = keep.tile([P, MT], F32, name="pos")
         nc.vector.tensor_copy(out=pos[:], in_=pos_i[:])

@@ -30,11 +30,10 @@ TWO_PI = 2.0 * math.pi
 C1 = 6.28125
 C2 = TWO_PI - C1
 
-X_SPLIT = ((0, 2), (2, 4), (4, 12))
-XP_SPLIT = ((0, 2), (2, 4), (4, 12))
+XP_SPLIT = ((0, 4), (4, 12))
 S_BUFS = 16
 MG = 4
-WARM_BEFORE, WARM_AFTER = 8, 14
+WARM_BEFORE, WARM_AFTER = 8, 8
 TAIL = 3
 
 
@@ -51,12 +50,12 @@ def tile_selfattention_pa_kernel(
         psum = ctx.enter_context(tc.psum_pool(name="psum", bufs=8))
         ctx.enter_context(tc.manual_schedule())
 
-        x_codes = [keep.tile([P, G, 256 * (m1 - m0)], U8, name="xc%d" % n, align_bytes=64)
-                   for n, (m0, m1) in enumerate(X_SPLIT)]
+        x_first = [keep.tile([P, 256 * MG], U8, name="xf%d" % g, align_bytes=64) for g in range(G)]
+        x_rest = keep.tile([P, G, 256 * (MT - MG)], U8, name="xr", align_bytes=64)
         x_planes = [keep.tile([P, G, 128 * (m1 - m0)], U8, name="xp%d" % n, align_bytes=64)
                     for n, (m0, m1) in enumerate(XP_SPLIT)]
         w0_codes = [None] + [keep.tile([P, G, 1024], U8, name="w0c%d" % b, align_bytes=64) for b in range(1, NB)]
-        w00_codes = [keep.tile([P, 2, 1024], U8, name="w00c%d" % n, align_bytes=64) for n in range(2)]
+        w00_codes = [keep.tile([P, 1024], U8, name="w00c%d" % g, align_bytes=64) for g in range(G)]
         w0_planes = [keep.tile([P, G, 512], U8, name="w0p%d" % b, align_bytes=64) for b in range(NB)]
         w_codes = [None] + [keep.tile([P, G, 2 * UW], U8, name="wc%d" % i, align_bytes=64) for i in range(1, NI)]
         w_planes = [None] + [keep.tile([P, G, UW], U8, name="wp%d" % i, align_bytes=64) for i in range(1, NI)]
@@ -81,7 +80,7 @@ def tile_selfattention_pa_kernel(
         nc.vector.memset(x_planes[0][:].bitcast(I32), 0)
         nc.vector.memset(b_rows[32:64, :], 0.0)
         nc.vector.memset(b_rows[64:128, :], 0.0)
-        for t in (w0_planes[0], x_planes[1], w0_planes[1], w0_planes[2], x_planes[2]):
+        for t in (w0_planes[0], w0_planes[1], w0_planes[2], x_planes[1]):
             nc.vector.memset(t[:].bitcast(I32), 0)
         make_identity(nc, ident[:])
         nc.gpsimd.iota(pos_i[:], pattern=[[P, MT]], base=0, channel_multiplier=1)
@@ -89,21 +88,23 @@ def tile_selfattention_pa_kernel(
         def load_bias(i):
             nc.gpsimd.dma_start(out=bias[i][:], in_=b_qkv[UW * i : UW * (i + 1)].partition_broadcast(P))
 
+        def load_pass(dst, src, g):
+            nc.sync.dma_start(out=dst[:].bitcast(I32), in_=src[g, :, 0:1024].bitcast(I32))
+
         nc.sync.dma_start(out=b_rows[0:32, :], in_=b_qkv.rearrange("(n c) -> n c", c=BW))
-        load_planes(x_planes[0], hidden_states_scales, 0, 128 * 2, 0, 2)
-        load_codes(x_codes[0], hidden_states_words, 0, 256 * 2)
-        load_codes(w00_codes[0], W_qkv_words, 0, 1024, 0, 2)
-        load_planes(x_planes[0], hidden_states_scales, 0, 128 * 2, 2, 4)
+        load_pass(x_first[0], hidden_states_words, 0)
+        load_pass(w00_codes[0], W_qkv_words, 0)
+        load_planes(x_planes[0], hidden_states_scales, 0, 128 * MG)
         load_planes(w0_planes[0], W_qkv_scales, 0, 512)
-        load_codes(w00_codes[1], W_qkv_words, 0, 1024, 2, 4)
-        load_codes(x_codes[1], hidden_states_words, 256 * 2, 256 * 4)
-        load_planes(x_planes[1], hidden_states_scales, 128 * 2, 128 * 4)
+        for g in range(1, G):
+            load_pass(x_first[g], hidden_states_words, g)
+            load_pass(w00_codes[g], W_qkv_words, g)
         load_planes(w0_planes[1], W_qkv_scales, 512, 1024)
         load_codes(w0_codes[1], W_qkv_words, 1024, 2048)
         load_planes(w0_planes[2], W_qkv_scales, 1024, 1536)
         load_codes(w0_codes[2], W_qkv_words, 2048, 3072)
-        load_planes(x_planes[2], hidden_states_scales, 128 * 4, 128 * 12)
-        load_codes(x_codes[2], hidden_states_words, 256 * 4, 256 * 12)
+        load_planes(x_planes[1], hidden_states_scales, 128 * MG, 128 * MT)
+        load_codes(x_rest, hidden_states_words, 256 * MG, 256 * MT)
 
         def keep_busy(n):
             idle = psum.tile([P, 512], F32, name="acc")
@@ -167,30 +168,35 @@ def tile_selfattention_pa_kernel(
         nc.scalar.activation(out=tab[:, :, 0, 0:HALF], in_=arg_cos[:], func=ACT.Sin)
         nc.scalar.activation(out=tab[:, :, 0, HALF:ROT], in_=arg_cos[:], func=ACT.Sin)
 
+        def one_pass(out, i, m, c0, width, g):
+            if m < MG:
+                xc = x_first[g][:, 256 * m : 256 * (m + 1)]
+                xp = x_planes[0][:, g, 128 * m : 128 * (m + 1)]
+            else:
+                xc = x_rest[:, g, 256 * (m - MG) : 256 * (m - MG + 1)]
+                xp = x_planes[1][:, g, 128 * (m - MG) : 128 * (m - MG + 1)]
+            if i == 0 and c0 == 0:
+                wc = w00_codes[g][:, :]
+                wp = w0_planes[0][:, g, :]
+            elif i == 0:
+                wc = w0_codes[c0 // 512][:, g, 2 * (c0 % 512) : 2 * (c0 % 512 + width)]
+                wp = w0_planes[c0 // 512][:, g, c0 % 512 : c0 % 512 + width]
+            else:
+                wc = w_codes[i][:, g, 2 * c0 : 2 * (c0 + width)]
+                wp = w_planes[i][:, g, c0 : c0 + width]
+            nc.tensor.matmul_mx(
+                out=out,
+                lhsT=xc.bitcast(FP4X4),
+                lhsT_scale=xp,
+                rhs=wc.bitcast(FP4X4),
+                rhs_scale=wp,
+                start=(g == 0),
+                stop=(g == G - 1),
+            )
+
         def multiply(out, i, m, c0, width):
-            n = [k for k, (m0, m1) in enumerate(X_SPLIT) if m0 <= m < m1][0]
-            mm = m - X_SPLIT[n][0]
-            np_ = [k for k, (m0, m1) in enumerate(XP_SPLIT) if m0 <= m < m1][0]
-            mp = m - XP_SPLIT[np_][0]
             for g in range(G):
-                if i == 0 and c0 == 0:
-                    wc = w00_codes[g // 2][:, g % 2, :]
-                    wp = w0_planes[0][:, g, :]
-                elif i == 0:
-                    wc = w0_codes[c0 // 512][:, g, 2 * (c0 % 512) : 2 * (c0 % 512 + width)]
-                    wp = w0_planes[c0 // 512][:, g, c0 % 512 : c0 % 512 + width]
-                else:
-                    wc = w_codes[i][:, g, 2 * c0 : 2 * (c0 + width)]
-                    wp = w_planes[i][:, g, c0 : c0 + width]
-                nc.tensor.matmul_mx(
-                    out=out,
-                    lhsT=x_codes[n][:, g, 256 * mm : 256 * (mm + 1)].bitcast(FP4X4),
-                    lhsT_scale=x_planes[np_][:, g, 128 * mp : 128 * (mp + 1)],
-                    rhs=wc.bitcast(FP4X4),
-                    rhs_scale=wp,
-                    start=(g == 0),
-                    stop=(g == G - 1),
-                )
+                one_pass(out, i, m, c0, width, g)
 
         stage = {}
 
@@ -202,6 +208,9 @@ def tile_selfattention_pa_kernel(
         def block(i, m, b):
             acc = psum.tile([P, 512], F32, name="acc")
             multiply(acc[:], i, m, 512 * b, 512)
+            empty(acc, i, m, b)
+
+        def empty(acc, i, m, b):
             st = staging(i, m)
             s = 0
             for step in range(4):
@@ -274,10 +283,17 @@ def tile_selfattention_pa_kernel(
             )
             store(nc.sync, i, m, 2, h0, h0 + 2)
 
+        accs = [psum.tile([P, 512], F32, name="acc") for m in range(MG)]
+        for g in range(G):
+            for m in range(MG):
+                one_pass(accs[m][:], 0, m, 0, 512, g)
+        for m in range(MG):
+            empty(accs[m], 0, m, 0)
         for m0 in range(0, MT, MG):
             for b in range(NB):
                 for m in range(m0, m0 + MG):
-                    block(0, m, b)
+                    if m0 + b > 0:
+                        block(0, m, b)
                     if b == NB - 1:
                         finish(0, m)
         for i in range(1, NI):

from contextlib import ExitStack
import math

import concourse.mybir as mybir
from concourse.masks import make_identity

SEQ, HID, NH, HD, ROT = 1536, 2048, 16, 128, 32
BASE = 10000.0
FLOPS = 2 * SEQ * HID * 3 * NH * HD

F32 = mybir.dt.float32
BF16 = mybir.dt.bfloat16
I32 = mybir.dt.int32
U8 = mybir.dt.uint8
FP4X4 = mybir.dt.float4_e2m1fn_x4
ALU = mybir.AluOpType
ACT = mybir.ActivationFunctionType

P = 128
G = HID // 512
MT = SEQ // P
NI = 4
HG = NH // NI
UW = 3 * HG * HD
NB = UW // 512
HALF = ROT // 2
BW = 3 * NH * HD // 32

TWO_PI = 2.0 * math.pi
C1 = 6.28125
C2 = TWO_PI - C1

XP_SPLIT = ((0, 4), (4, 12))
S_BUFS = 16
MG = 4
WARM_BEFORE, WARM_AFTER = 8, 8
TAIL = 3


def tile_selfattention_pa_kernel(
    tc, hidden_states_words, hidden_states_scales, W_qkv_words, W_qkv_scales, b_qkv, out_0, out_1, out_2
):
    nc = tc.nc
    outs = [o.rearrange("s b h d -> (s b) (h d)") for o in (out_0, out_1, out_2)]

    with ExitStack() as ctx:
        keep = ctx.enter_context(tc.tile_pool(name="keep", bufs=1))
        spool = ctx.enter_context(tc.tile_pool(name="spool", bufs=S_BUFS))
        tpool = ctx.enter_context(tc.tile_pool(name="tpool", bufs=2))
        psum = ctx.enter_context(tc.psum_pool(name="psum", bufs=8))
        ctx.enter_context(tc.manual_schedule())

        x_first = [keep.tile([P, 256 * MG], U8, name="xf%d" % g, align_bytes=64) for g in range(G)]
        x_rest = keep.tile([P, G, 256 * (MT - MG)], U8, name="xr", align_bytes=64)
        x_planes = [keep.tile([P, G, 128 * (m1 - m0)], U8, name="xp%d" % n, align_bytes=64)
                    for n, (m0, m1) in enumerate(XP_SPLIT)]
        w0_codes = [None] + [keep.tile([P, G, 1024], U8, name="w0c%d" % b, align_bytes=64) for b in range(1, NB)]
        w00_codes = [keep.tile([P, 1024], U8, name="w00c%d" % g, align_bytes=64) for g in range(G)]
        w0_planes = [keep.tile([P, G, 512], U8, name="w0p%d" % b, align_bytes=64) for b in range(NB)]
        w_codes = [None] + [keep.tile([P, G, 2 * UW], U8, name="wc%d" % i, align_bytes=64) for i in range(1, NI)]
        w_planes = [None] + [keep.tile([P, G, UW], U8, name="wp%d" % i, align_bytes=64) for i in range(1, NI)]
        bias = [keep.tile([P, UW], F32, name="bias0")] + [keep.tile([P, UW], BF16, name="bias%d" % i) for i in range(1, NI)]
        b_rows = keep.tile([P, BW], BF16, name="b_rows")
        ident = keep.tile([P, P], BF16, name="ident")
        pos_i = keep.tile([P, MT], I32, name="pos_i")

        def load_codes(dst, src, c0, c1, g0=0, g1=G):
            nc.sync.dma_start(
                out=dst[:].bitcast(I32),
                in_=src[g0:g1, :, c0:c1].rearrange("g p n -> p g n").bitcast(I32),
            )

        def load_planes(dst, src, c0, c1, q0=0, q1=4):
            for q in range(q0, q1):
                nc.sync.dma_start(
                    out=dst[32 * q : 32 * q + 4, :, :].bitcast(I32),
                    in_=src[:, 4 * q : 4 * q + 4, c0:c1].rearrange("g r n -> r g n").bitcast(I32),
                )

        nc.vector.memset(x_planes[0][:].bitcast(I32), 0)
        nc.vector.memset(b_rows[32:64, :], 0.0)
        nc.vector.memset(b_rows[64:128, :], 0.0)
        for t in (w0_planes[0], w0_planes[1], w0_planes[2], x_planes[1]):
            nc.vector.memset(t[:].bitcast(I32), 0)
        make_identity(nc, ident[:])
        nc.gpsimd.iota(pos_i[:], pattern=[[P, MT]], base=0, channel_multiplier=1)

        def load_bias(i):
            nc.gpsimd.dma_start(out=bias[i][:], in_=b_qkv[UW * i : UW * (i + 1)].partition_broadcast(P))

        def load_pass(dst, src, g):
            nc.sync.dma_start(out=dst[:].bitcast(I32), in_=src[g, :, 0:1024].bitcast(I32))

        nc.sync.dma_start(out=b_rows[0:32, :], in_=b_qkv.rearrange("(n c) -> n c", c=BW))
        load_pass(x_first[0], hidden_states_words, 0)
        load_pass(w00_codes[0], W_qkv_words, 0)
        load_planes(x_planes[0], hidden_states_scales, 0, 128 * MG)
        load_planes(w0_planes[0], W_qkv_scales, 0, 512)
        for g in range(1, G):
            load_pass(x_first[g], hidden_states_words, g)
            load_pass(w00_codes[g], W_qkv_words, g)
        load_planes(w0_planes[1], W_qkv_scales, 512, 1024)
        load_codes(w0_codes[1], W_qkv_words, 1024, 2048)
        load_planes(w0_planes[2], W_qkv_scales, 1024, 1536)
        load_codes(w0_codes[2], W_qkv_words, 2048, 3072)
        load_planes(x_planes[1], hidden_states_scales, 128 * MG, 128 * MT)
        load_codes(x_rest, hidden_states_words, 256 * MG, 256 * MT)

        def keep_busy(n):
            idle = psum.tile([P, 512], F32, name="acc")
            for k in range(n):
                nc.tensor.matmul(out=idle[:, 0:P], lhsT=ident[:], rhs=ident[:], start=True, stop=True)

        keep_busy(WARM_BEFORE)
        for b in range(UW // (2 * BW)):
            acc = psum.tile([P, 512], F32, name="acc")
            for e in range(2):
                nc.tensor.matmul(
                    out=acc[:, BW * e : BW * (e + 1)],
                    lhsT=ident[:, 2 * b + e : 2 * b + e + 1].to_broadcast([P, P]),
                    rhs=b_rows[:],
                    start=True,
                    stop=True,
                )
            nc.scalar.copy(out=bias[0][:, 2 * BW * b : 2 * BW * (b + 1)], in_=acc[:, 0 : 2 * BW])
        keep_busy(WARM_AFTER)

        pos = keep.tile([P, MT], F32, name="pos")
        nc.vector.tensor_copy(out=pos[:], in_=pos_i[:])
        ang = keep.tile([P, MT, HALF], F32, name="ang")
        for j in range(HALF):
            nc.vector.tensor_scalar(
                out=ang[:, :, j], in0=pos[:], scalar1=BASE ** (-j / float(HALF)), scalar2=None, op0=ALU.mult
            )
        turns_i = keep.tile([P, MT, HALF], I32, name="turns_i")
        nc.vector.tensor_scalar(out=turns_i[:], in0=ang[:], scalar1=1.0 / TWO_PI, scalar2=None, op0=ALU.mult)
        turns = keep.tile([P, MT, HALF], F32, name="turns")
        nc.vector.tensor_copy(out=turns[:], in_=turns_i[:])
        red1 = keep.tile([P, MT, HALF], F32, name="red1")
        nc.vector.scalar_tensor_tensor(out=red1[:], in0=turns[:], scalar=-C1, in1=ang[:], op0=ALU.mult, op1=ALU.add)
        red2 = keep.tile([P, MT, HALF], F32, name="red2")
        nc.vector.scalar_tensor_tensor(out=red2[:], in0=turns[:], scalar=-C2, in1=red1[:], op0=ALU.mult, op1=ALU.add)

        def wrapped(eng, src, name, bound, op, shift):
            fix = keep.tile([P, MT, HALF], F32, name=name + "f")
            eng.tensor_scalar(out=fix[:], in0=src[:], scalar1=bound, scalar2=shift, op0=op, op1=ALU.mult)
            res = keep.tile([P, MT, HALF], F32, name=name)
            eng.tensor_tensor(out=res[:], in0=src[:], in1=fix[:], op=ALU.add)
            return res

        arg_sin = wrapped(
            nc.vector, wrapped(nc.vector, red2, "sa", math.pi, ALU.is_gt, -TWO_PI), "sb", -math.pi, ALU.is_lt, TWO_PI
        )
        shifted = keep.tile([P, MT, HALF], F32, name="shifted")
        nc.gpsimd.tensor_scalar(out=shifted[:], in0=arg_sin[:], scalar1=1.0, scalar2=0.5 * math.pi, op0=ALU.mult, op1=ALU.add)
        arg_cos = wrapped(nc.gpsimd, shifted, "ca", math.pi, ALU.is_gt, -TWO_PI)
        load_bias(1)
        for i in range(1, NI):
            nc.gpsimd.memset(w_planes[i][:].bitcast(F32), 0.0)
        for i in range(1, NI):
            load_planes(w_planes[i], W_qkv_scales, UW * i, UW * (i + 1))
        for i in range(1, NI):
            load_codes(w_codes[i], W_qkv_words, 2 * UW * i, 2 * UW * (i + 1))

        tab = keep.tile([P, MT, 2, ROT], F32, name="tab")
        nc.scalar.activation(out=tab[:, :, 1, 0:HALF], in_=arg_sin[:], func=ACT.Sin)
        nc.scalar.activation(out=tab[:, :, 1, HALF:ROT], in_=arg_sin[:], func=ACT.Sin, scale=-1.0)
        nc.scalar.activation(out=tab[:, :, 0, 0:HALF], in_=arg_cos[:], func=ACT.Sin)
        nc.scalar.activation(out=tab[:, :, 0, HALF:ROT], in_=arg_cos[:], func=ACT.Sin)

        def one_pass(out, i, m, c0, width, g):
            if m < MG:
                xc = x_first[g][:, 256 * m : 256 * (m + 1)]
                xp = x_planes[0][:, g, 128 * m : 128 * (m + 1)]
            else:
                xc = x_rest[:, g, 256 * (m - MG) : 256 * (m - MG + 1)]
                xp = x_planes[1][:, g, 128 * (m - MG) : 128 * (m - MG + 1)]
            if i == 0 and c0 == 0:
                wc = w00_codes[g][:, :]
                wp = w0_planes[0][:, g, :]
            elif i == 0:
                wc = w0_codes[c0 // 512][:, g, 2 * (c0 % 512) : 2 * (c0 % 512 + width)]
                wp = w0_planes[c0 // 512][:, g, c0 % 512 : c0 % 512 + width]
            else:
                wc = w_codes[i][:, g, 2 * c0 : 2 * (c0 + width)]
                wp = w_planes[i][:, g, c0 : c0 + width]
            nc.tensor.matmul_mx(
                out=out,
                lhsT=xc.bitcast(FP4X4),
                lhsT_scale=xp,
                rhs=wc.bitcast(FP4X4),
                rhs_scale=wp,
                start=(g == 0),
                stop=(g == G - 1),
            )

        def multiply(out, i, m, c0, width):
            for g in range(G):
                one_pass(out, i, m, c0, width, g)

        stage = {}

        def staging(i, m):
            if (i, m) not in stage:
                stage[(i, m)] = spool.tile([P, 3, HG, HD], F32, name="st")
            return stage[(i, m)]

        def block(i, m, b):
            acc = psum.tile([P, 512], F32, name="acc")
            multiply(acc[:], i, m, 512 * b, 512)
            empty(acc, i, m, b)

        def empty(acc, i, m, b):
            st = staging(i, m)
            s = 0
            for step in range(4):
                if s < 4:
                    h, c = divmod(4 * b + s, 3)
                    n = min(3 - c, 4 - s)
                    nc.vector.tensor_tensor(
                        out=st[:, c : c + n, h, :],
                        in0=acc[:, HD * s : HD * (s + n)].rearrange("p (c d) -> p c d", c=n),
                        in1=bias[i][:, 512 * b + HD * s : 512 * b + HD * (s + n)].rearrange("p (c d) -> p c d", c=n),
                        op=ALU.add,
                    )
                    s += n

        def rotate(i, m):
            st = staging(i, m)
            rot = st[:, 0:2, :, :].rearrange("p c h d -> p (c h) d")[:, :, 0:ROT]
            prod = tpool.tile([P, 2 * HG, 2, ROT], F32, name="prod")
            nc.gpsimd.tensor_tensor(
                out=prod[:],
                in0=rot.unsqueeze(2).to_broadcast([P, 2 * HG, 2, ROT]),
                in1=tab[:, m, :, :].unsqueeze(1).to_broadcast([P, 2 * HG, 2, ROT]),
                op=ALU.mult,
            )
            nc.gpsimd.tensor_tensor(
                out=rot[:, :, 0:HALF], in0=prod[:, :, 0, 0:HALF], in1=prod[:, :, 1, HALF:ROT], op=ALU.add
            )
            nc.gpsimd.tensor_tensor(
                out=rot[:, :, HALF:ROT], in0=prod[:, :, 0, HALF:ROT], in1=prod[:, :, 1, 0:HALF], op=ALU.add
            )

        def store(queue, i, m, c, h0, h1):
            nc_rows = slice(P * m, P * (m + 1))
            queue.dma_start(
                out=outs[c][nc_rows, HD * (HG * i + h0) : HD * (HG * i + h1)],
                in_=staging(i, m)[:, c, h0:h1, :].rearrange("p h d -> p (h d)"),
            )

        def finish(i, m):
            rotate(i, m)
            if m == 0 and i + 2 < NI:
                load_bias(i + 2)
            store(nc.sync, i, m, 2, 0, HG)
            store(nc.scalar, i, m, 0, 0, HG)
            store(nc.scalar, i, m, 1, 0, HG)

        def by_head(ap, h0):
            return ap[:, 3 * HD * h0 : 3 * HD * (h0 + 2)].rearrange("p (h x) -> p h x", h=2)

        def qk_pair(i, m, h0):
            acc = psum.tile([P, 512], F32, name="acc")
            for hh in range(2):
                multiply(acc[:, 256 * hh : 256 * (hh + 1)], i, m, 3 * HD * (h0 + hh), 2 * HD)
            nc.vector.tensor_tensor(
                out=staging(i, m)[:, 0:2, h0 : h0 + 2, :].rearrange("p c h d -> p h c d"),
                in0=acc[:].rearrange("p (h c d) -> p h c d", h=2, c=2),
                in1=by_head(bias[i], h0)[:, :, 0 : 2 * HD].rearrange("p h (c d) -> p h c d", c=2),
                op=ALU.add,
            )

        def v_pair(i, m, h0):
            acc = psum.tile([P, 512], F32, name="acc")
            for hh in range(2):
                multiply(acc[:, HD * hh : HD * (hh + 1)], i, m, 3 * HD * (h0 + hh) + 2 * HD, HD)
            nc.vector.tensor_tensor(
                out=staging(i, m)[:, 2, h0 : h0 + 2, :],
                in0=acc[:, 0 : 2 * HD].rearrange("p (h d) -> p h d", h=2),
                in1=by_head(bias[i], h0)[:, :, 2 * HD : 3 * HD],
                op=ALU.add,
            )
            store(nc.sync, i, m, 2, h0, h0 + 2)

        accs = [psum.tile([P, 512], F32, name="acc") for m in range(MG)]
        for g in range(G):
            for m in range(MG):
                one_pass(accs[m][:], 0, m, 0, 512, g)
        for m in range(MG):
            empty(accs[m], 0, m, 0)
        for m0 in range(0, MT, MG):
            for b in range(NB):
                for m in range(m0, m0 + MG):
                    if m0 + b > 0:
                        block(0, m, b)
                    if b == NB - 1:
                        finish(0, m)
        for i in range(1, NI):
            for m in range(MT - TAIL if i == NI - 1 else MT):
                for b in range(NB):
                    block(i, m, b)
                finish(i, m)
        for m in range(MT - TAIL, MT):
            for h0 in range(0, HG, 2):
                qk_pair(NI - 1, m, h0)
            rotate(NI - 1, m)
            store(nc.scalar, NI - 1, m, 0, 0, HG)
            store(nc.scalar, NI - 1, m, 1, 0, HG)
        for m in range(MT - TAIL, MT):
            for h0 in range(0, HG, 2):
                v_pair(NI - 1, m, h0)
